import numpy as np
import ml_dtypes


def mxq(x, axis, fmt="e4m3"):
    dtype, down = {"e4m3": (ml_dtypes.float8_e4m3fn, 7), "e5m2": (ml_dtypes.float8_e5m2, 14)}[fmt]
    v = np.moveaxis(np.asarray(x, np.float32).astype(ml_dtypes.bfloat16).astype(np.float64), axis, -1)
    blocks = v.reshape(v.shape[:-1] + (-1, 32))
    amax = np.abs(blocks).max(-1, keepdims=True)
    byte = np.maximum(np.where(amax > 0, np.frexp(amax)[1] - 1 + 127, 0) - down, 1)
    scale = np.exp2(byte - 127.0)
    codes = (blocks / scale).astype(np.float32).astype(dtype).astype(np.float64)
    return np.moveaxis((codes * scale).reshape(v.shape), -1, axis)


WIDE = False


def mx_kscale(k):
    if not WIDE:
        return np.ones(k)
    levels = np.array([10, -10, 5, -5, 0])
    a = np.random.permutation(np.resize(levels, k // 512 * 4)).reshape(k // 512, 4)
    idx = np.arange(k)
    return np.exp2(a[idx // 512, idx % 128 // 32])


BF16 = ml_dtypes.bfloat16


def bf(x):
    return np.asarray(x, np.float32).astype(BF16)


def f64(x):
    return np.asarray(x).astype(np.float64)


B, V, H, CD = 4096, 1024, 512, 1


def sigmoid(x):
    return 0.5 * (1.0 + np.tanh(0.5 * x))


def setup_inputs():
    s = mx_kscale(V)
    s = s / s.min()
    return {"v": bf(np.random.uniform(size=(B, V)) * s),
            "w": bf(np.random.standard_normal((V, H)) * 1.5 / np.sqrt(V) / s[:, None]),
            "vb": bf(np.random.standard_normal(V) * 0.5 / s),
            "hb": bf(np.random.standard_normal(H) * 0.3)}


def reference(v, w, vb, hb):
    v, w = f64(v), f64(w)
    h_p = sigmoid(f64(hb) + (mxq(v, 1, "e4m3") @ mxq(w, 0, "e4m3")))
    v_prediction = sigmoid(f64(vb) + (mxq(h_p, 1, "e4m3") @ mxq(w.T, 0, "e4m3")))
    return h_p, v_prediction

@@ -1,0 +1,289 @@
+from contextlib import ExitStack
+
+import concourse.mybir as mybir
+from concourse.masks import make_identity
+
+F32 = mybir.dt.float32
+BF16 = mybir.dt.bfloat16
+U32 = mybir.dt.uint32
+U8 = mybir.dt.uint8
+FP8X4 = mybir.dt.float8_e4m3fn_x4
+SIGMOID = mybir.ActivationFunctionType.Sigmoid
+ADD = mybir.AluOpType.add
+
+B, V, H = 4096, 1024, 512
+FLOPS = 2 * B * V * H * 2
+
+P = 128
+PACK = 4
+K_PASS = P * PACK
+BANK = 512
+ROW_TILES = B // P
+CHUNK_TILES = BANK // P
+CHUNKS = ROW_TILES // CHUNK_TILES
+V_PASSES = V // K_PASS
+H_BLOCKS = H // P
+V_HALVES = V // BANK
+UNITS = ROW_TILES
+
+LAG_MM1 = 6
+LAG_MM2 = LAG_MM1 + 5
+LAG_W2 = 4
+STEPS = UNITS + LAG_MM2 + 2
+
+
+def tile_rbm_pa_t_kernel(tc, v, w, vb, hb, out_0, out_1):
+    nc = tc.nc
+    v_by_tile = v.rearrange("(p t) k -> p t k", t=ROW_TILES)
+    h_by_tile = out_0.rearrange("(p t) k -> p t k", t=ROW_TILES)
+    r_by_tile = out_1.rearrange("(p t) k -> p t k", t=ROW_TILES)
+
+    with ExitStack() as stack:
+        const = stack.enter_context(tc.tile_pool(name="const", bufs=1))
+        ring = stack.enter_context(tc.tile_pool(name="ring", bufs=3))
+        psum = stack.enter_context(tc.psum_pool(name="psum", bufs=2))
+        stack.enter_context(tc.manual_schedule())
+
+        hb_rows = const.tile([P, P], BF16, name="hb_rows")
+        nc.vector.memset(hb_rows[:], 0.0)
+        nc.scalar.dma_start(out=hb_rows[0:H_BLOCKS, :], in_=hb.rearrange("(t c) -> t c", c=P))
+        vb_rows = const.tile([P, V], BF16, name="vb_rows")
+        nc.vector.memset(vb_rows[:], 0.0)
+        nc.scalar.dma_start(out=vb_rows[0:1, :], in_=vb.rearrange("(o c) -> o c", o=1))
+        ones = const.tile([P, P], BF16, name="ones")
+        nc.vector.memset(ones[:], 1.0)
+        warm = const.tile([P, 1], F32, name="warm")
+        nc.vector.memset(warm[:], 0.0)
+        nc.scalar.activation(out=warm[:], in_=warm[:], func=SIGMOID)
+
+        w_pairs = const.tile([P, V_PASSES, PACK, H], BF16, name="w_pairs")
+        for g in range(V_PASSES):
+            nc.sync.dma_start(
+                out=w_pairs[:, g, :, :].rearrange("q (u e) c -> q u (e c)", e=2),
+                in_=w[g * K_PASS : (g + 1) * K_PASS, :].rearrange("(u q e) c -> q u (e c)", u=2, e=2),
+            )
+        v_rows = []
+        for c in range(CHUNKS):
+            v_chunk = const.tile([P, CHUNK_TILES, V], BF16, name="v_rows%d" % c)
+            nc.sync.dma_start(out=v_chunk[:], in_=v_by_tile[:, c * CHUNK_TILES : (c + 1) * CHUNK_TILES, :])
+            v_rows.append(v_chunk)
+
+        ident_f32 = const.tile([P, P], F32, name="ident_f32")
+        make_identity(nc, ident_f32[:])
+        ident_bf16 = const.tile([P, P], BF16, name="ident_bf16")
+        make_identity(nc, ident_bf16[:])
+
+        w1_grouped = const.tile([P, V_PASSES, H * PACK], BF16, name="w1_grouped", align_bytes=64)
+        w1_codes = const.tile([P, V_PASSES, H], U32, name="w1_codes", align_bytes=64)
+        w1_scales = const.tile([P, V_PASSES, H], U8, name="w1_scales", align_bytes=64)
+        for g in range(V_PASSES):
+            nc.vector.tensor_copy(
+                out=w1_grouped[:, g, :].rearrange("p (c t) -> p c t", t=PACK),
+                in_=w_pairs[:, g, :, :].rearrange("p t c -> p c t"),
+            )
+        for g in range(V_PASSES):
+            nc.vector.quantize_mx(
+                out=w1_codes[:, g, :].bitcast(FP8X4), scales=w1_scales[:, g, :], in_=w1_grouped[:, g, :]
+            )
+
+        w2_grouped = const.tile([P, V * PACK], BF16, name="w2_grouped", align_bytes=64)
+        w2_codes = const.tile([P, V], U32, name="w2_codes", align_bytes=64)
+        w2_scales = const.tile([P, V], U8, name="w2_scales", align_bytes=64)
+        for x in range(2 * V_PASSES):
+            g, u = divmod(x, 2)
+            w2_bank = psum.tile([P, H_BLOCKS, 2, P], BF16, name="w2_bank", tag="ht")
+            for t in range(H_BLOCKS):
+                for e in range(2):
+                    nc.tensor.transpose(
+                        out=w2_bank[:, t, e, :],
+                        in_=w_pairs[:, g, 2 * u + e, t * P : (t + 1) * P],
+                        identity=ident_bf16[:],
+                    )
+            width = 2 * P * PACK
+            nc.scalar.copy(
+                out=w2_grouped[:, x * width : (x + 1) * width].rearrange("p (q e t) -> p q e t", e=2, t=PACK),
+                in_=w2_bank[:].rearrange("p t e q -> p q e t"),
+            )
+
+        def quantise_w2(n):
+            if not 0 <= n < V_HALVES:
+                return
+            nc.vector.quantize_mx(
+                out=w2_codes[:, n * BANK : (n + 1) * BANK].bitcast(FP8X4),
+                scales=w2_scales[:, n * BANK : (n + 1) * BANK],
+                in_=w2_grouped[:, n * BANK * PACK : (n + 1) * BANK * PACK],
+            )
+
+        hb_t = psum.tile([P, P], BF16, name="hb_t", tag="m1")
+        nc.tensor.transpose(out=hb_t[:], in_=hb_rows[:], identity=ident_bf16[:])
+        hb_col = const.tile([P, H_BLOCKS], F32, name="hb_col")
+        nc.vector.tensor_copy(out=hb_col[:], in_=hb_t[:, 0:H_BLOCKS])
+
+        vb_all = const.tile([P, V], F32, name="vb_all")
+
+        def broadcast_vb(n):
+            if not 0 <= n < V_HALVES:
+                return
+            cols = slice(n * BANK, (n + 1) * BANK)
+            vb_bank = psum.tile([P, BANK], F32, name="vb_bank", tag="m2")
+            nc.tensor.matmul(out=vb_bank[:], lhsT=ones[:], rhs=vb_rows[:, cols], start=True, stop=True)
+            nc.vector.tensor_copy(out=vb_all[:, cols], in_=vb_bank[:])
+
+        v_bank, v_grouped, v_codes, v_scales = {}, {}, {}, {}
+        m1_bank, h_t, h_grouped, h_codes, h_scales = {}, {}, {}, {}, {}
+        h_bank, h_out, m2_bank, r_out = {}, {}, {}, {}
+
+        def transpose_v(x):
+            if not 0 <= x < UNITS:
+                return
+            c, r = divmod(x, CHUNK_TILES)
+            half, g = divmod(r, V_PASSES)
+            words = v_rows[c][:].bitcast(F32)
+            v_bank[x] = psum.tile([P, 2, 2 * P], F32, name="v_bank", tag="vt")
+            for j in range(2):
+                for u in range(2):
+                    first = (2 * g + u) * P
+                    nc.tensor.transpose(
+                        out=v_bank[x][:, u, j * P : (j + 1) * P],
+                        in_=words[:, 2 * half + j, first : first + P],
+                        identity=ident_f32[:],
+                    )
+
+        def evacuate_v(x, engine_copy):
+            if not 0 <= x < UNITS:
+                return
+            v_grouped[x] = ring.tile([P, 2 * P * PACK], BF16, name="v_grouped", tag="v_grouped", align_bytes=64)
+            engine_copy(
+                out=v_grouped[x][:].bitcast(F32).rearrange("p (n u) -> p n u", u=2),
+                in_=v_bank[x][:].rearrange("p u n -> p n u"),
+            )
+
+        def quantise_v(x):
+            if not 0 <= x < UNITS:
+                return
+            c, r = divmod(x, CHUNK_TILES)
+            half, g = divmod(r, V_PASSES)
+            if r == 0:
+                v_codes[c] = ring.tile([P, V_PASSES, BANK], U32, name="v_codes", tag="v_codes", align_bytes=64)
+                v_scales[c] = ring.tile([P, V_PASSES, BANK], U8, name="v_scales", tag="v_scales", align_bytes=64)
+            cols = slice(half * 2 * P, (half + 1) * 2 * P)
+            nc.vector.quantize_mx(
+                out=v_codes[c][:, g, cols].bitcast(FP8X4), scales=v_scales[c][:, g, cols], in_=v_grouped[x][:]
+            )
+
+        def first_matmul(x):
+            if not 0 <= x < UNITS:
+                return
+            c, t = divmod(x, H_BLOCKS)
+            m1_bank[x] = psum.tile([P, BANK], F32, name="m1_bank", tag="m1")
+            for g in range(V_PASSES):
+                nc.tensor.matmul_mx(
+                    out=m1_bank[x][:],
+                    lhsT=w1_codes[:, g, t * P : (t + 1) * P].bitcast(FP8X4),
+                    lhsT_scale=w1_scales[:, g, t * P : (t + 1) * P],
+                    rhs=v_codes[c][:, g, :].bitcast(FP8X4),
+                    rhs_scale=v_scales[c][:, g, :],
+                    start=(g == 0),
+                    stop=(g == V_PASSES - 1),
+                )
+
+        def hidden_sigmoid(x):
+            if not 0 <= x < UNITS:
+                return
+            c, t = divmod(x, H_BLOCKS)
+            if t == 0:
+                h_t[c] = ring.tile([P, H_BLOCKS, BANK], F32, name="h_t", tag="h_t")
+            nc.scalar.activation(out=h_t[c][:, t, :], in_=m1_bank[x][:], func=SIGMOID, bias=hb_col[:, t : t + 1])
+
+        def regroup_h(x):
+            if not 0 <= x < UNITS:
+                return
+            c, j = divmod(x, CHUNK_TILES)
+            h_grouped[x] = ring.tile([P, P * PACK], BF16, name="h_grouped", tag="h_grouped", align_bytes=64)
+            nc.vector.tensor_copy(
+                out=h_grouped[x][:].rearrange("p (n t) -> p n t", t=PACK),
+                in_=h_t[c][:, :, j * P : (j + 1) * P].rearrange("p t n -> p n t"),
+            )
+
+        def quantise_h(x):
+            if not 0 <= x < UNITS:
+                return
+            h_codes[x] = ring.tile([P, P], U32, name="h_codes", tag="h_codes", align_bytes=64)
+            h_scales[x] = ring.tile([P, P], U8, name="h_scales", tag="h_scales", align_bytes=64)
+            nc.vector.quantize_mx(out=h_codes[x][:].bitcast(FP8X4), scales=h_scales[x][:], in_=h_grouped[x][:])
+
+        def transpose_h(x):
+            if not 0 <= x < UNITS:
+                return
+            c, j = divmod(x, CHUNK_TILES)
+            h_bank[x] = psum.tile([P, H], F32, name="h_bank", tag="ht")
+            for t in range(H_BLOCKS):
+                nc.tensor.transpose(
+                    out=h_bank[x][:, t * P : (t + 1) * P],
+                    in_=h_t[c][:, t, j * P : (j + 1) * P],
+                    identity=ident_f32[:],
+                )
+
+        def evacuate_h(x, engine_copy):
+            if not 0 <= x < UNITS:
+                return
+            c, j = divmod(x, CHUNK_TILES)
+            if j == 0:
+                h_out[c] = ring.tile([P, CHUNK_TILES, H], F32, name="h_out", tag="h_out")
+            engine_copy(out=h_out[c][:, j, :], in_=h_bank[x][:])
+            if j == CHUNK_TILES - 1:
+                nc.sync.dma_start(out=h_by_tile[:, c * CHUNK_TILES : (c + 1) * CHUNK_TILES, :], in_=h_out[c][:])
+
+        def second_matmul(x):
+            if not 0 <= x < UNITS:
+                return
+            for n in range(V_HALVES):
+                m2_bank[x, n] = psum.tile([P, BANK], F32, name="m2_bank", tag="m2")
+                nc.tensor.matmul_mx(
+                    out=m2_bank[x, n][:],
+                    lhsT=h_codes[x][:].bitcast(FP8X4),
+                    lhsT_scale=h_scales[x][:],
+                    rhs=w2_codes[:, n * BANK : (n + 1) * BANK].bitcast(FP8X4),
+                    rhs_scale=w2_scales[:, n * BANK : (n + 1) * BANK],
+                    start=True,
+                    stop=True,
+                )
+
+        def add_visible_bias(x):
+            if not 0 <= x < UNITS:
+                return
+            r_out[x] = ring.tile([P, V], F32, name="r_out", tag="r_out", bufs=6)
+            for n in range(V_HALVES):
+                cols = slice(n * BANK, (n + 1) * BANK)
+                nc.vector.tensor_tensor(out=r_out[x][:, cols], in0=m2_bank[x, n][:], in1=vb_all[:, cols], op=ADD)
+
+        def visible_sigmoid(x):
+            if not 0 <= x < UNITS:
+                return
+            nc.scalar.activation(out=r_out[x][:], in_=r_out[x][:], func=SIGMOID)
+            nc.sync.dma_start(out=r_by_tile[:, x, :], in_=r_out[x][:])
+
+        for s in range(STEPS):
+            filling = s < LAG_MM2 - 1
+            draining = s >= UNITS
+            first_matmul(s - LAG_MM1)
+            second_matmul(s - LAG_MM2)
+            transpose_v(s)
+            transpose_h(s - LAG_MM2)
+            scalar_takes_h = draining or (s - LAG_MM2) % CHUNK_TILES == CHUNK_TILES - 1
+            if not filling:
+                evacuate_v(s, nc.scalar.copy)
+            hidden_sigmoid(s - LAG_MM1)
+            if scalar_takes_h:
+                evacuate_h(s - LAG_MM2, nc.scalar.copy)
+            visible_sigmoid(s - LAG_MM2 - 1)
+            regroup_h(s - LAG_MM2 + 1)
+            add_visible_bias(s - LAG_MM2)
+            quantise_h(s - LAG_MM2 + 1)
+            if not scalar_takes_h:
+                evacuate_h(s - LAG_MM2, nc.vector.tensor_copy)
+            if filling:
+                evacuate_v(s, nc.vector.tensor_copy)
+            quantise_v(s - 1)
+            quantise_w2(s - LAG_W2)
+            broadcast_vb(s - LAG_MM1)

@@ -10,6 +10,7 @@ U8 = mybir.dt.uint8
 FP8X4 = mybir.dt.float8_e4m3fn_x4
 SIGMOID = mybir.ActivationFunctionType.Sigmoid
 ADD = mybir.AluOpType.add
+MULT = mybir.AluOpType.mult
 
 B, V, H = 4096, 1024, 512
 FLOPS = 2 * B * V * H * 2
@@ -199,10 +200,14 @@ def tile_rbm_pa_t_kernel(tc, v, w, vb, hb, out_0, out_1):
             if not 0 <= x < UNITS:
                 return
             c, j = divmod(x, CHUNK_TILES)
-            h_grouped[x] = ring.tile([P, P * PACK], BF16, name="h_grouped", tag="h_grouped", align_bytes=64)
-            nc.vector.tensor_copy(
+            h_grouped[x] = ring.tile([P, P * PACK], BF16, name="h_grouped", tag="h_grouped", bufs=1, align_bytes=64)
+            nc.gpsimd.tensor_scalar(
                 out=h_grouped[x][:].rearrange("p (n t) -> p n t", t=PACK),
-                in_=h_t[c][:, :, j * P : (j + 1) * P].rearrange("p t n -> p n t"),
+                in0=h_t[c][:, :, j * P : (j + 1) * P].rearrange("p t n -> p n t"),
+                scalar1=1.0,
+                scalar2=0.0,
+                op0=MULT,
+                op1=ADD,
             )
 
         def quantise_h(x):
@@ -224,15 +229,15 @@ def tile_rbm_pa_t_kernel(tc, v, w, vb, hb, out_0, out_1):
                     identity=ident_f32[:],
                 )
 
-        def evacuate_h(x, engine_copy):
+        def evacuate_h(x):
             if not 0 <= x < UNITS:
                 return
-            c, j = divmod(x, CHUNK_TILES)
+            pair, j = divmod(x, 2)
             if j == 0:
-                h_out[c] = ring.tile([P, CHUNK_TILES, H], F32, name="h_out", tag="h_out")
-            engine_copy(out=h_out[c][:, j, :], in_=h_bank[x][:])
-            if j == CHUNK_TILES - 1:
-                nc.sync.dma_start(out=h_by_tile[:, c * CHUNK_TILES : (c + 1) * CHUNK_TILES, :], in_=h_out[c][:])
+                h_out[pair] = ring.tile([P, 2, H], F32, name="h_out", tag="h_out")
+            nc.vector.tensor_copy(out=h_out[pair][:, j, :], in_=h_bank[x][:])
+            if j == 1:
+                nc.sync.dma_start(out=h_by_tile[:, 2 * pair : 2 * pair + 2, :], in_=h_out[pair][:])
 
         def second_matmul(x):
             if not 0 <= x < UNITS:
@@ -264,26 +269,21 @@ def tile_rbm_pa_t_kernel(tc, v, w, vb, hb, out_0, out_1):
             nc.sync.dma_start(out=r_by_tile[:, x, :], in_=r_out[x][:])
 
         for s in range(STEPS):
-            filling = s < LAG_MM2 - 1
-            draining = s >= UNITS
+            filling = s < LAG_MM2
             first_matmul(s - LAG_MM1)
             second_matmul(s - LAG_MM2)
             transpose_v(s)
             transpose_h(s - LAG_MM2)
-            scalar_takes_h = draining or (s - LAG_MM2) % CHUNK_TILES == CHUNK_TILES - 1
             if not filling:
                 evacuate_v(s, nc.scalar.copy)
             hidden_sigmoid(s - LAG_MM1)
-            if scalar_takes_h:
-                evacuate_h(s - LAG_MM2, nc.scalar.copy)
             visible_sigmoid(s - LAG_MM2 - 1)
-            regroup_h(s - LAG_MM2 + 1)
-            add_visible_bias(s - LAG_MM2)
-            quantise_h(s - LAG_MM2 + 1)
-            if not scalar_takes_h:
-                evacuate_h(s - LAG_MM2, nc.vector.tensor_copy)
             if filling:
                 evacuate_v(s, nc.vector.tensor_copy)
             quantise_v(s - 1)
             quantise_w2(s - LAG_W2)
+            quantise_h(s - LAG_MM2 + 1)
+            add_visible_bias(s - LAG_MM2)
+            evacuate_h(s - LAG_MM2)
             broadcast_vb(s - LAG_MM1)
+            regroup_h(s - LAG_MM2 + 2)

@@ -150,11 +150,11 @@ def tile_rbm_pa_t_kernel(tc, v, w, vb, hb, out_0, out_1):
                         identity=ident_f32[:],
                     )
 
-        def evacuate_v(x, engine_copy):
+        def evacuate_v(x):
             if not 0 <= x < UNITS:
                 return
             v_grouped[x] = ring.tile([P, 2 * P * PACK], BF16, name="v_grouped", tag="v_grouped", align_bytes=64)
-            engine_copy(
+            nc.scalar.copy(
                 out=v_grouped[x][:].bitcast(F32).rearrange("p (n u) -> p n u", u=2),
                 in_=v_bank[x][:].rearrange("p u n -> p n u"),
             )
@@ -229,13 +229,13 @@ def tile_rbm_pa_t_kernel(tc, v, w, vb, hb, out_0, out_1):
                     identity=ident_f32[:],
                 )
 
-        def evacuate_h(x):
+        def evacuate_h(x, engine_copy):
             if not 0 <= x < UNITS:
                 return
             pair, j = divmod(x, 2)
             if j == 0:
                 h_out[pair] = ring.tile([P, 2, H], F32, name="h_out", tag="h_out")
-            nc.vector.tensor_copy(out=h_out[pair][:, j, :], in_=h_bank[x][:])
+            engine_copy(out=h_out[pair][:, j, :], in_=h_bank[x][:])
             if j == 1:
                 nc.sync.dma_start(out=h_by_tile[:, 2 * pair : 2 * pair + 2, :], in_=h_out[pair][:])
 
@@ -269,21 +269,21 @@ def tile_rbm_pa_t_kernel(tc, v, w, vb, hb, out_0, out_1):
             nc.sync.dma_start(out=r_by_tile[:, x, :], in_=r_out[x][:])
 
         for s in range(STEPS):
-            filling = s < LAG_MM2
-            first_matmul(s - LAG_MM1)
-            second_matmul(s - LAG_MM2)
             transpose_v(s)
             transpose_h(s - LAG_MM2)
-            if not filling:
-                evacuate_v(s, nc.scalar.copy)
+            first_matmul(s - LAG_MM1)
+            second_matmul(s - LAG_MM2)
+            scalar_has_time = s >= UNITS + LAG_MM1
+            evacuate_v(s)
             hidden_sigmoid(s - LAG_MM1)
+            if scalar_has_time:
+                evacuate_h(s - LAG_MM2, nc.scalar.copy)
             visible_sigmoid(s - LAG_MM2 - 1)
-            if filling:
-                evacuate_v(s, nc.vector.tensor_copy)
             quantise_v(s - 1)
             quantise_w2(s - LAG_W2)
             quantise_h(s - LAG_MM2 + 1)
+            if not scalar_has_time:
+                evacuate_h(s - LAG_MM2, nc.vector.tensor_copy)
             add_visible_bias(s - LAG_MM2)
-            evacuate_h(s - LAG_MM2)
             broadcast_vb(s - LAG_MM1)
             regroup_h(s - LAG_MM2 + 2)

@@ -27,7 +27,7 @@ H_BLOCKS = H // P
 V_HALVES = V // BANK
 UNITS = ROW_TILES
 
-LAG_MM1 = 6
+LAG_MM1 = 5
 LAG_MM2 = LAG_MM1 + 5
 LAG_W2 = 4
 STEPS = UNITS + LAG_MM2 + 2
@@ -42,7 +42,7 @@ def tile_rbm_pa_t_kernel(tc, v, w, vb, hb, out_0, out_1):
     with ExitStack() as stack:
         const = stack.enter_context(tc.tile_pool(name="const", bufs=1))
         ring = stack.enter_context(tc.tile_pool(name="ring", bufs=3))
-        psum = stack.enter_context(tc.psum_pool(name="psum", bufs=2))
+        psum = stack.enter_context(tc.psum_pool(name="psum", bufs=8))
         stack.enter_context(tc.manual_schedule())
 
         hb_rows = const.tile([P, P], BF16, name="hb_rows")
@@ -92,7 +92,7 @@ def tile_rbm_pa_t_kernel(tc, v, w, vb, hb, out_0, out_1):
         w2_scales = const.tile([P, V], U8, name="w2_scales", align_bytes=64)
         for x in range(2 * V_PASSES):
             g, u = divmod(x, 2)
-            w2_bank = psum.tile([P, H_BLOCKS, 2, P], BF16, name="w2_bank", tag="ht")
+            w2_bank = psum.tile([P, H_BLOCKS, 2, P], BF16, name="w2_bank", tag="bank")
             for t in range(H_BLOCKS):
                 for e in range(2):
                     nc.tensor.transpose(
@@ -115,7 +115,7 @@ def tile_rbm_pa_t_kernel(tc, v, w, vb, hb, out_0, out_1):
                 in_=w2_grouped[:, n * BANK * PACK : (n + 1) * BANK * PACK],
             )
 
-        hb_t = psum.tile([P, P], BF16, name="hb_t", tag="m1")
+        hb_t = psum.tile([P, P], BF16, name="hb_t", tag="bank")
         nc.tensor.transpose(out=hb_t[:], in_=hb_rows[:], identity=ident_bf16[:])
         hb_col = const.tile([P, H_BLOCKS], F32, name="hb_col")
         nc.vector.tensor_copy(out=hb_col[:], in_=hb_t[:, 0:H_BLOCKS])
@@ -126,7 +126,7 @@ def tile_rbm_pa_t_kernel(tc, v, w, vb, hb, out_0, out_1):
             if not 0 <= n < V_HALVES:
                 return
             cols = slice(n * BANK, (n + 1) * BANK)
-            vb_bank = psum.tile([P, BANK], F32, name="vb_bank", tag="m2")
+            vb_bank = psum.tile([P, BANK], F32, name="vb_bank", tag="bank")
             nc.tensor.matmul(out=vb_bank[:], lhsT=ones[:], rhs=vb_rows[:, cols], start=True, stop=True)
             nc.vector.tensor_copy(out=vb_all[:, cols], in_=vb_bank[:])
 
@@ -140,7 +140,7 @@ def tile_rbm_pa_t_kernel(tc, v, w, vb, hb, out_0, out_1):
             c, r = divmod(x, CHUNK_TILES)
             half, g = divmod(r, V_PASSES)
             words = v_rows[c][:].bitcast(F32)
-            v_bank[x] = psum.tile([P, 2, 2 * P], F32, name="v_bank", tag="vt")
+            v_bank[x] = psum.tile([P, 2, 2 * P], F32, name="v_bank", tag="bank")
             for j in range(2):
                 for u in range(2):
                     first = (2 * g + u) * P
@@ -176,7 +176,7 @@ def tile_rbm_pa_t_kernel(tc, v, w, vb, hb, out_0, out_1):
             if not 0 <= x < UNITS:
                 return
             c, t = divmod(x, H_BLOCKS)
-            m1_bank[x] = psum.tile([P, BANK], F32, name="m1_bank", tag="m1")
+            m1_bank[x] = psum.tile([P, BANK], F32, name="m1_bank", tag="bank")
             for g in range(V_PASSES):
                 nc.tensor.matmul_mx(
                     out=m1_bank[x][:],
@@ -221,7 +221,7 @@ def tile_rbm_pa_t_kernel(tc, v, w, vb, hb, out_0, out_1):
             if not 0 <= x < UNITS:
                 return
             c, j = divmod(x, CHUNK_TILES)
-            h_bank[x] = psum.tile([P, H], F32, name="h_bank", tag="ht")
+            h_bank[x] = psum.tile([P, H], F32, name="h_bank", tag="bank")
             for t in range(H_BLOCKS):
                 nc.tensor.transpose(
                     out=h_bank[x][:, t * P : (t + 1) * P],
@@ -243,7 +243,7 @@ def tile_rbm_pa_t_kernel(tc, v, w, vb, hb, out_0, out_1):
             if not 0 <= x < UNITS:
                 return
             for n in range(V_HALVES):
-                m2_bank[x, n] = psum.tile([P, BANK], F32, name="m2_bank", tag="m2")
+                m2_bank[x, n] = psum.tile([P, BANK], F32, name="m2_bank", tag="bank")
                 nc.tensor.matmul_mx(
                     out=m2_bank[x, n][:],
                     lhsT=h_codes[x][:].bitcast(FP8X4),

@@ -27,10 +27,27 @@ H_BLOCKS = H // P
 V_HALVES = V // BANK
 UNITS = ROW_TILES
 
-LAG_MM1 = 5
-LAG_MM2 = LAG_MM1 + 5
-LAG_W2 = 4
-STEPS = UNITS + LAG_MM2 + 2
+FAST = 2 * CHUNK_TILES
+
+
+def step_of_v(x):
+    return x // 2 if x < FAST else x - FAST // 2
+
+
+def step_of_m1(x):
+    return step_of_v(CHUNK_TILES - 1) + 2 + x // 2 if x < H_BLOCKS else x + 1
+
+
+def step_of_m2(x):
+    return step_of_m1(H_BLOCKS - 1) + 2 + x
+
+
+def units_at(step_of, s):
+    return [x for x in range(UNITS) if step_of(x) == s]
+
+
+LAG_W2 = 2
+STEPS = step_of_m2(UNITS - 1) + 2
 
 
 def tile_rbm_pa_t_kernel(tc, v, w, vb, hb, out_0, out_1):
@@ -74,6 +91,17 @@ def tile_rbm_pa_t_kernel(tc, v, w, vb, hb, out_0, out_1):
         ident_bf16 = const.tile([P, P], BF16, name="ident_bf16")
         make_identity(nc, ident_bf16[:])
 
+        hb_t = psum.tile([P, P], BF16, name="hb_t", tag="bank")
+        nc.tensor.transpose(out=hb_t[:], in_=hb_rows[:], identity=ident_bf16[:])
+        hb_col = const.tile([P, H_BLOCKS], F32, name="hb_col")
+        nc.vector.tensor_copy(out=hb_col[:], in_=hb_t[:, 0:H_BLOCKS])
+        vb_all = const.tile([P, V], F32, name="vb_all")
+        for n in range(V_HALVES):
+            cols = slice(n * BANK, (n + 1) * BANK)
+            vb_bank = psum.tile([P, BANK], F32, name="vb_bank", tag="bank")
+            nc.tensor.matmul(out=vb_bank[:], lhsT=ones[:], rhs=vb_rows[:, cols], start=True, stop=True)
+            nc.vector.tensor_copy(out=vb_all[:, cols], in_=vb_bank[:])
+
         w1_grouped = const.tile([P, V_PASSES, H * PACK], BF16, name="w1_grouped", align_bytes=64)
         w1_codes = const.tile([P, V_PASSES, H], U32, name="w1_codes", align_bytes=64)
         w1_scales = const.tile([P, V_PASSES, H], U8, name="w1_scales", align_bytes=64)
@@ -115,20 +143,6 @@ def tile_rbm_pa_t_kernel(tc, v, w, vb, hb, out_0, out_1):
                 in_=w2_grouped[:, n * BANK * PACK : (n + 1) * BANK * PACK],
             )
 
-        hb_t = psum.tile([P, P], BF16, name="hb_t", tag="bank")
-        nc.tensor.transpose(out=hb_t[:], in_=hb_rows[:], identity=ident_bf16[:])
-        hb_col = const.tile([P, H_BLOCKS], F32, name="hb_col")
-        nc.vector.tensor_copy(out=hb_col[:], in_=hb_t[:, 0:H_BLOCKS])
-
-        vb_all = const.tile([P, V], F32, name="vb_all")
-
-        def broadcast_vb(n):
-            if not 0 <= n < V_HALVES:
-                return
-            cols = slice(n * BANK, (n + 1) * BANK)
-            vb_bank = psum.tile([P, BANK], F32, name="vb_bank", tag="bank")
-            nc.tensor.matmul(out=vb_bank[:], lhsT=ones[:], rhs=vb_rows[:, cols], start=True, stop=True)
-            nc.vector.tensor_copy(out=vb_all[:, cols], in_=vb_bank[:])
 
         v_bank, v_grouped, v_codes, v_scales = {}, {}, {}, {}
         m1_bank, h_t, h_grouped, h_codes, h_scales = {}, {}, {}, {}, {}
@@ -150,11 +164,11 @@ def tile_rbm_pa_t_kernel(tc, v, w, vb, hb, out_0, out_1):
                         identity=ident_f32[:],
                     )
 
-        def evacuate_v(x):
+        def evacuate_v(x, engine_copy):
             if not 0 <= x < UNITS:
                 return
             v_grouped[x] = ring.tile([P, 2 * P * PACK], BF16, name="v_grouped", tag="v_grouped", align_bytes=64)
-            nc.scalar.copy(
+            engine_copy(
                 out=v_grouped[x][:].bitcast(F32).rearrange("p (n u) -> p n u", u=2),
                 in_=v_bank[x][:].rearrange("p u n -> p n u"),
             )
@@ -268,22 +282,41 @@ def tile_rbm_pa_t_kernel(tc, v, w, vb, hb, out_0, out_1):
             nc.scalar.activation(out=r_out[x][:], in_=r_out[x][:], func=SIGMOID)
             nc.sync.dma_start(out=r_by_tile[:, x, :], in_=r_out[x][:])
 
+        def vector_empties_v(x):
+            return CHUNK_TILES <= x < FAST and x % 2 == 1
+
         for s in range(STEPS):
-            transpose_v(s)
-            transpose_h(s - LAG_MM2)
-            first_matmul(s - LAG_MM1)
-            second_matmul(s - LAG_MM2)
-            scalar_has_time = s >= UNITS + LAG_MM1
-            evacuate_v(s)
-            hidden_sigmoid(s - LAG_MM1)
+            for x in units_at(step_of_v, s):
+                transpose_v(x)
+            for x in units_at(step_of_m2, s):
+                transpose_h(x)
+            for x in units_at(step_of_m1, s):
+                first_matmul(x)
+            for x in units_at(step_of_m2, s):
+                second_matmul(x)
+            scalar_has_time = s > step_of_m1(UNITS - 1)
+            for x in units_at(step_of_v, s):
+                if not vector_empties_v(x):
+                    evacuate_v(x, nc.scalar.copy)
+            for x in units_at(step_of_m1, s):
+                hidden_sigmoid(x)
             if scalar_has_time:
-                evacuate_h(s - LAG_MM2, nc.scalar.copy)
-            visible_sigmoid(s - LAG_MM2 - 1)
-            quantise_v(s - 1)
+                for x in units_at(step_of_m2, s):
+                    evacuate_h(x, nc.scalar.copy)
+            for x in units_at(step_of_m2, s - 1):
+                visible_sigmoid(x)
+            for x in units_at(step_of_v, s - 1):
+                quantise_v(x)
             quantise_w2(s - LAG_W2)
-            quantise_h(s - LAG_MM2 + 1)
+            for x in units_at(step_of_m2, s + 1):
+                quantise_h(x)
+            for x in units_at(step_of_v, s):
+                if vector_empties_v(x):
+                    evacuate_v(x, nc.vector.tensor_copy)
             if not scalar_has_time:
-                evacuate_h(s - LAG_MM2, nc.vector.tensor_copy)
-            add_visible_bias(s - LAG_MM2)
-            broadcast_vb(s - LAG_MM1)
-            regroup_h(s - LAG_MM2 + 2)
+                for x in units_at(step_of_m2, s):
+                    evacuate_h(x, nc.vector.tensor_copy)
+            for x in units_at(step_of_m2, s):
+                add_visible_bias(x)
+            for x in units_at(step_of_m2, s + 2):
+                regroup_h(x)

@@ -31,22 +31,22 @@ FAST = 2 * CHUNK_TILES
 
 
 def step_of_v(x):
-    return x // 2 if x < FAST else x - FAST // 2
+    return x // 2 if x < FAST else x - FAST // 2 - 1
 
 
 def step_of_m1(x):
-    return step_of_v(CHUNK_TILES - 1) + 2 + x // 2 if x < H_BLOCKS else x + 1
+    return step_of_v(CHUNK_TILES - 1) + 1 + x // 2 if x < H_BLOCKS else x + 1
 
 
 def step_of_m2(x):
-    return step_of_m1(H_BLOCKS - 1) + 2 + x
+    return x + 6
 
 
 def units_at(step_of, s):
     return [x for x in range(UNITS) if step_of(x) == s]
 
 
-LAG_W2 = 2
+FIRST_W2_STEP = 3
 STEPS = step_of_m2(UNITS - 1) + 2
 
 
@@ -62,14 +62,8 @@ def tile_rbm_pa_t_kernel(tc, v, w, vb, hb, out_0, out_1):
         psum = stack.enter_context(tc.psum_pool(name="psum", bufs=8))
         stack.enter_context(tc.manual_schedule())
 
-        hb_rows = const.tile([P, P], BF16, name="hb_rows")
-        nc.vector.memset(hb_rows[:], 0.0)
-        nc.scalar.dma_start(out=hb_rows[0:H_BLOCKS, :], in_=hb.rearrange("(t c) -> t c", c=P))
-        vb_rows = const.tile([P, V], BF16, name="vb_rows")
-        nc.vector.memset(vb_rows[:], 0.0)
-        nc.scalar.dma_start(out=vb_rows[0:1, :], in_=vb.rearrange("(o c) -> o c", o=1))
-        ones = const.tile([P, P], BF16, name="ones")
-        nc.vector.memset(ones[:], 1.0)
+        hb_col = const.tile([P, H_BLOCKS], BF16, name="hb_col")
+        vb_all = const.tile([P, V], BF16, name="vb_all")
         warm = const.tile([P, 1], F32, name="warm")
         nc.vector.memset(warm[:], 0.0)
         nc.scalar.activation(out=warm[:], in_=warm[:], func=SIGMOID)
@@ -80,36 +74,33 @@ def tile_rbm_pa_t_kernel(tc, v, w, vb, hb, out_0, out_1):
                 out=w_pairs[:, g, :, :].rearrange("q (u e) c -> q u (e c)", e=2),
                 in_=w[g * K_PASS : (g + 1) * K_PASS, :].rearrange("(u q e) c -> q u (e c)", u=2, e=2),
             )
+        nc.sync.dma_start(out=hb_col[:].rearrange("p (u e) -> p u e", u=2), in_=hb.rearrange("(u p e) -> p u e", u=2, e=2))
         v_rows = []
         for c in range(CHUNKS):
             v_chunk = const.tile([P, CHUNK_TILES, V], BF16, name="v_rows%d" % c)
-            nc.sync.dma_start(out=v_chunk[:], in_=v_by_tile[:, c * CHUNK_TILES : (c + 1) * CHUNK_TILES, :])
+            size = CHUNK_TILES // 2 if c == 0 else CHUNK_TILES
+            for j in range(0, CHUNK_TILES, size):
+                first = c * CHUNK_TILES + j
+                nc.sync.dma_start(out=v_chunk[:, j : j + size, :], in_=v_by_tile[:, first : first + size, :])
             v_rows.append(v_chunk)
+            if c == 2:
+                nc.sync.dma_start(out=vb_all[:], in_=vb.partition_broadcast(P))
 
         ident_f32 = const.tile([P, P], F32, name="ident_f32")
         make_identity(nc, ident_f32[:])
-        ident_bf16 = const.tile([P, P], BF16, name="ident_bf16")
-        make_identity(nc, ident_bf16[:])
-
-        hb_t = psum.tile([P, P], BF16, name="hb_t", tag="bank")
-        nc.tensor.transpose(out=hb_t[:], in_=hb_rows[:], identity=ident_bf16[:])
-        hb_col = const.tile([P, H_BLOCKS], F32, name="hb_col")
-        nc.vector.tensor_copy(out=hb_col[:], in_=hb_t[:, 0:H_BLOCKS])
-        vb_all = const.tile([P, V], F32, name="vb_all")
-        for n in range(V_HALVES):
-            cols = slice(n * BANK, (n + 1) * BANK)
-            vb_bank = psum.tile([P, BANK], F32, name="vb_bank", tag="bank")
-            nc.tensor.matmul(out=vb_bank[:], lhsT=ones[:], rhs=vb_rows[:, cols], start=True, stop=True)
-            nc.vector.tensor_copy(out=vb_all[:, cols], in_=vb_bank[:])
 
         w1_grouped = const.tile([P, V_PASSES, H * PACK], BF16, name="w1_grouped", align_bytes=64)
         w1_codes = const.tile([P, V_PASSES, H], U32, name="w1_codes", align_bytes=64)
         w1_scales = const.tile([P, V_PASSES, H], U8, name="w1_scales", align_bytes=64)
         for g in range(V_PASSES):
-            nc.vector.tensor_copy(
-                out=w1_grouped[:, g, :].rearrange("p (c t) -> p c t", t=PACK),
-                in_=w_pairs[:, g, :, :].rearrange("p t c -> p c t"),
-            )
+            for u in range(2):
+                half = slice(u * 2 * P, (u + 1) * 2 * P)
+                nc.vector.tensor_copy(
+                    out=w1_grouped[:, g, u * 2 * P * PACK : (u + 1) * 2 * P * PACK].rearrange(
+                        "p (e q t) -> p e q t", e=2, t=PACK
+                    ),
+                    in_=w_pairs[:, g, :, half].rearrange("p t (q e) -> p e q t", e=2),
+                )
         for g in range(V_PASSES):
             nc.vector.quantize_mx(
                 out=w1_codes[:, g, :].bitcast(FP8X4), scales=w1_scales[:, g, :], in_=w1_grouped[:, g, :]
@@ -119,19 +110,20 @@ def tile_rbm_pa_t_kernel(tc, v, w, vb, hb, out_0, out_1):
         w2_codes = const.tile([P, V], U32, name="w2_codes", align_bytes=64)
         w2_scales = const.tile([P, V], U8, name="w2_scales", align_bytes=64)
         for x in range(2 * V_PASSES):
-            g, u = divmod(x, 2)
-            w2_bank = psum.tile([P, H_BLOCKS, 2, P], BF16, name="w2_bank", tag="bank")
-            for t in range(H_BLOCKS):
-                for e in range(2):
+            g, r = divmod(x, 2)
+            words = w_pairs[:, g, 2 * r : 2 * r + 2, :].bitcast(F32)
+            w2_bank = psum.tile([P, 2, 2, P], F32, name="w2_bank", tag="bank")
+            for e in range(2):
+                for u in range(2):
                     nc.tensor.transpose(
-                        out=w2_bank[:, t, e, :],
-                        in_=w_pairs[:, g, 2 * u + e, t * P : (t + 1) * P],
-                        identity=ident_bf16[:],
+                        out=w2_bank[:, e, u, :],
+                        in_=words[:, e, u * P : (u + 1) * P],
+                        identity=ident_f32[:],
                     )
             width = 2 * P * PACK
             nc.scalar.copy(
-                out=w2_grouped[:, x * width : (x + 1) * width].rearrange("p (q e t) -> p q e t", e=2, t=PACK),
-                in_=w2_bank[:].rearrange("p t e q -> p q e t"),
+                out=w2_grouped[:, x * width : (x + 1) * width].bitcast(F32).rearrange("p (q e u) -> p q e u", e=2, u=2),
+                in_=w2_bank[:].rearrange("p e u q -> p q e u"),
             )
 
         def quantise_w2(n):
@@ -142,7 +134,6 @@ def tile_rbm_pa_t_kernel(tc, v, w, vb, hb, out_0, out_1):
                 scales=w2_scales[:, n * BANK : (n + 1) * BANK],
                 in_=w2_grouped[:, n * BANK * PACK : (n + 1) * BANK * PACK],
             )
-
 
         v_bank, v_grouped, v_codes, v_scales = {}, {}, {}, {}
         m1_bank, h_t, h_grouped, h_codes, h_scales = {}, {}, {}, {}, {}
@@ -249,7 +240,10 @@ def tile_rbm_pa_t_kernel(tc, v, w, vb, hb, out_0, out_1):
             pair, j = divmod(x, 2)
             if j == 0:
                 h_out[pair] = ring.tile([P, 2, H], F32, name="h_out", tag="h_out")
-            engine_copy(out=h_out[pair][:, j, :], in_=h_bank[x][:])
+            engine_copy(
+                out=h_out[pair][:, j, :].rearrange("p (u q e) -> p u q e", u=2, e=2),
+                in_=h_bank[x][:].rearrange("p (u e q) -> p u q e", u=2, e=2),
+            )
             if j == 1:
                 nc.sync.dma_start(out=h_by_tile[:, 2 * pair : 2 * pair + 2, :], in_=h_out[pair][:])
 
@@ -283,21 +277,26 @@ def tile_rbm_pa_t_kernel(tc, v, w, vb, hb, out_0, out_1):
             nc.sync.dma_start(out=r_by_tile[:, x, :], in_=r_out[x][:])
 
         def vector_empties_v(x):
-            return CHUNK_TILES <= x < FAST and x % 2 == 1
+            return x < FAST and x % 2 == 1
 
         for s in range(STEPS):
+            scalar_has_time = s > step_of_m1(UNITS - 1)
             for x in units_at(step_of_v, s):
                 transpose_v(x)
             for x in units_at(step_of_m2, s):
                 transpose_h(x)
+            for x in units_at(step_of_v, s):
+                if not vector_empties_v(x):
+                    evacuate_v(x, nc.scalar.copy)
+            for x in units_at(step_of_v, s - 1):
+                quantise_v(x)
+            quantise_w2(s - FIRST_W2_STEP)
+            for x in units_at(step_of_m2, s + 1):
+                quantise_h(x)
             for x in units_at(step_of_m1, s):
                 first_matmul(x)
             for x in units_at(step_of_m2, s):
                 second_matmul(x)
-            scalar_has_time = s > step_of_m1(UNITS - 1)
-            for x in units_at(step_of_v, s):
-                if not vector_empties_v(x):
-                    evacuate_v(x, nc.scalar.copy)
             for x in units_at(step_of_m1, s):
                 hidden_sigmoid(x)
             if scalar_has_time:
@@ -305,11 +304,6 @@ def tile_rbm_pa_t_kernel(tc, v, w, vb, hb, out_0, out_1):
                     evacuate_h(x, nc.scalar.copy)
             for x in units_at(step_of_m2, s - 1):
                 visible_sigmoid(x)
-            for x in units_at(step_of_v, s - 1):
-                quantise_v(x)
-            quantise_w2(s - LAG_W2)
-            for x in units_at(step_of_m2, s + 1):
-                quantise_h(x)
             for x in units_at(step_of_v, s):
                 if vector_empties_v(x):
                     evacuate_v(x, nc.vector.tensor_copy)

@@ -63,7 +63,11 @@ def tile_rbm_pa_t_kernel(tc, v, w, vb, hb, out_0, out_1):
         stack.enter_context(tc.manual_schedule())
 
         hb_col = const.tile([P, H_BLOCKS], BF16, name="hb_col")
-        vb_all = const.tile([P, V], BF16, name="vb_all")
+        vb_rows = const.tile([P, V], BF16, name="vb_rows")
+        nc.vector.memset(vb_rows[:], 0.0)
+        vb_all = const.tile([P, V], F32, name="vb_all")
+        ones = const.tile([P, P], BF16, name="ones")
+        nc.vector.memset(ones[:], 1.0)
         warm = const.tile([P, 1], F32, name="warm")
         nc.vector.memset(warm[:], 0.0)
         nc.scalar.activation(out=warm[:], in_=warm[:], func=SIGMOID)
@@ -75,6 +79,7 @@ def tile_rbm_pa_t_kernel(tc, v, w, vb, hb, out_0, out_1):
                 in_=w[g * K_PASS : (g + 1) * K_PASS, :].rearrange("(u q e) c -> q u (e c)", u=2, e=2),
             )
         nc.sync.dma_start(out=hb_col[:].rearrange("p (u e) -> p u e", u=2), in_=hb.rearrange("(u p e) -> p u e", u=2, e=2))
+        nc.sync.dma_start(out=vb_rows[0:1, :], in_=vb.rearrange("(o c) -> o c", o=1))
         v_rows = []
         for c in range(CHUNKS):
             v_chunk = const.tile([P, CHUNK_TILES, V], BF16, name="v_rows%d" % c)
@@ -83,8 +88,6 @@ def tile_rbm_pa_t_kernel(tc, v, w, vb, hb, out_0, out_1):
                 first = c * CHUNK_TILES + j
                 nc.sync.dma_start(out=v_chunk[:, j : j + size, :], in_=v_by_tile[:, first : first + size, :])
             v_rows.append(v_chunk)
-            if c == 2:
-                nc.sync.dma_start(out=vb_all[:], in_=vb.partition_broadcast(P))
 
         ident_f32 = const.tile([P, P], F32, name="ident_f32")
         make_identity(nc, ident_f32[:])
@@ -125,6 +128,13 @@ def tile_rbm_pa_t_kernel(tc, v, w, vb, hb, out_0, out_1):
                 out=w2_grouped[:, x * width : (x + 1) * width].bitcast(F32).rearrange("p (q e u) -> p q e u", e=2, u=2),
                 in_=w2_bank[:].rearrange("p e u q -> p q e u"),
             )
+
+        def broadcast_vb():
+            for n in range(V_HALVES):
+                cols = slice(n * BANK, (n + 1) * BANK)
+                vb_bank = psum.tile([P, BANK], F32, name="vb_bank", tag="bank")
+                nc.tensor.matmul(out=vb_bank[:], lhsT=ones[:], rhs=vb_rows[:, cols], start=True, stop=True)
+                nc.scalar.copy(out=vb_all[:, cols], in_=vb_bank[:])
 
         def quantise_w2(n):
             if not 0 <= n < V_HALVES:
@@ -288,6 +298,8 @@ def tile_rbm_pa_t_kernel(tc, v, w, vb, hb, out_0, out_1):
             for x in units_at(step_of_v, s):
                 if not vector_empties_v(x):
                     evacuate_v(x, nc.scalar.copy)
+            if s == 1:
+                broadcast_vb()
             for x in units_at(step_of_v, s - 1):
                 quantise_v(x)
             quantise_w2(s - FIRST_W2_STEP)

@@ -62,6 +62,8 @@ def tile_rbm_pa_t_kernel(tc, v, w, vb, hb, out_0, out_1):
         psum = stack.enter_context(tc.psum_pool(name="psum", bufs=8))
         stack.enter_context(tc.manual_schedule())
 
+        hb_rows = const.tile([P, 2 * P], BF16, name="hb_rows")
+        nc.vector.memset(hb_rows[:], 0.0)
         hb_col = const.tile([P, H_BLOCKS], BF16, name="hb_col")
         vb_rows = const.tile([P, V], BF16, name="vb_rows")
         nc.vector.memset(vb_rows[:], 0.0)
@@ -78,12 +80,12 @@ def tile_rbm_pa_t_kernel(tc, v, w, vb, hb, out_0, out_1):
                 out=w_pairs[:, g, :, :].rearrange("q (u e) c -> q u (e c)", e=2),
                 in_=w[g * K_PASS : (g + 1) * K_PASS, :].rearrange("(u q e) c -> q u (e c)", u=2, e=2),
             )
-        nc.sync.dma_start(out=hb_col[:].rearrange("p (u e) -> p u e", u=2), in_=hb.rearrange("(u p e) -> p u e", u=2, e=2))
+        nc.sync.dma_start(out=hb_rows[0:2, :], in_=hb.rearrange("(u c) -> u c", u=2))
         nc.sync.dma_start(out=vb_rows[0:1, :], in_=vb.rearrange("(o c) -> o c", o=1))
         v_rows = []
         for c in range(CHUNKS):
             v_chunk = const.tile([P, CHUNK_TILES, V], BF16, name="v_rows%d" % c)
-            size = CHUNK_TILES // 2 if c == 0 else CHUNK_TILES
+            size = CHUNK_TILES // 2 if c < 3 else CHUNK_TILES
             for j in range(0, CHUNK_TILES, size):
                 first = c * CHUNK_TILES + j
                 nc.sync.dma_start(out=v_chunk[:, j : j + size, :], in_=v_by_tile[:, first : first + size, :])
@@ -128,6 +130,10 @@ def tile_rbm_pa_t_kernel(tc, v, w, vb, hb, out_0, out_1):
                 out=w2_grouped[:, x * width : (x + 1) * width].bitcast(F32).rearrange("p (q e u) -> p q e u", e=2, u=2),
                 in_=w2_bank[:].rearrange("p e u q -> p q e u"),
             )
+
+        hb_bank = psum.tile([P, P], F32, name="hb_bank", tag="bank")
+        nc.tensor.transpose(out=hb_bank[:], in_=hb_rows[:].bitcast(F32), identity=ident_f32[:])
+        nc.scalar.copy(out=hb_col[:].bitcast(F32), in_=hb_bank[:, 0:2])
 
         def broadcast_vb():
             for n in range(V_HALVES):
@@ -287,7 +293,7 @@ def tile_rbm_pa_t_kernel(tc, v, w, vb, hb, out_0, out_1):
             nc.sync.dma_start(out=r_by_tile[:, x, :], in_=r_out[x][:])
 
         def vector_empties_v(x):
-            return x < FAST and x % 2 == 1
+            return CHUNK_TILES <= x < FAST and x % 2 == 1
 
         for s in range(STEPS):
             scalar_has_time = s > step_of_m1(UNITS - 1)
@@ -298,6 +304,9 @@ def tile_rbm_pa_t_kernel(tc, v, w, vb, hb, out_0, out_1):
             for x in units_at(step_of_v, s):
                 if not vector_empties_v(x):
                     evacuate_v(x, nc.scalar.copy)
+            if not scalar_has_time:
+                for x in units_at(step_of_m2, s):
+                    evacuate_h(x, nc.vector.tensor_copy)
             if s == 1:
                 broadcast_vb()
             for x in units_at(step_of_v, s - 1):
@@ -319,9 +328,6 @@ def tile_rbm_pa_t_kernel(tc, v, w, vb, hb, out_0, out_1):
             for x in units_at(step_of_v, s):
                 if vector_empties_v(x):
                     evacuate_v(x, nc.vector.tensor_copy)
-            if not scalar_has_time:
-                for x in units_at(step_of_m2, s):
-                    evacuate_h(x, nc.vector.tensor_copy)
             for x in units_at(step_of_m2, s):
                 add_visible_bias(x)
             for x in units_at(step_of_m2, s + 2):

from contextlib import ExitStack

import concourse.mybir as mybir
from concourse.masks import make_identity

F32 = mybir.dt.float32
BF16 = mybir.dt.bfloat16
U32 = mybir.dt.uint32
U8 = mybir.dt.uint8
FP8X4 = mybir.dt.float8_e4m3fn_x4
SIGMOID = mybir.ActivationFunctionType.Sigmoid
ADD = mybir.AluOpType.add
MULT = mybir.AluOpType.mult

B, V, H = 4096, 1024, 512
FLOPS = 2 * B * V * H * 2

P = 128
PACK = 4
K_PASS = P * PACK
BANK = 512
ROW_TILES = B // P
CHUNK_TILES = BANK // P
CHUNKS = ROW_TILES // CHUNK_TILES
V_PASSES = V // K_PASS
H_BLOCKS = H // P
V_HALVES = V // BANK
UNITS = ROW_TILES

FAST = 2 * CHUNK_TILES


def step_of_v(x):
    return x // 2 if x < FAST else x - FAST // 2 - 1


def step_of_m1(x):
    return step_of_v(CHUNK_TILES - 1) + 1 + x // 2 if x < H_BLOCKS else x + 1


def step_of_m2(x):
    return x + 6


def units_at(step_of, s):
    return [x for x in range(UNITS) if step_of(x) == s]


FIRST_W2_STEP = 3
STEPS = step_of_m2(UNITS - 1) + 2


def tile_rbm_pa_t_kernel(tc, v, w, vb, hb, out_0, out_1):
    nc = tc.nc
    v_by_tile = v.rearrange("(p t) k -> p t k", t=ROW_TILES)
    h_by_tile = out_0.rearrange("(p t) k -> p t k", t=ROW_TILES)
    r_by_tile = out_1.rearrange("(p t) k -> p t k", t=ROW_TILES)

    with ExitStack() as stack:
        const = stack.enter_context(tc.tile_pool(name="const", bufs=1))
        ring = stack.enter_context(tc.tile_pool(name="ring", bufs=3))
        psum = stack.enter_context(tc.psum_pool(name="psum", bufs=8))
        stack.enter_context(tc.manual_schedule())

        hb_rows = const.tile([P, 2 * P], BF16, name="hb_rows")
        nc.vector.memset(hb_rows[:], 0.0)
        hb_col = const.tile([P, H_BLOCKS], BF16, name="hb_col")
        vb_rows = const.tile([P, V], BF16, name="vb_rows")
        nc.vector.memset(vb_rows[:], 0.0)
        vb_all = const.tile([P, V], F32, name="vb_all")
        ones = const.tile([P, P], BF16, name="ones")
        nc.vector.memset(ones[:], 1.0)
        warm = const.tile([P, 1], F32, name="warm")
        nc.vector.memset(warm[:], 0.0)
        nc.scalar.activation(out=warm[:], in_=warm[:], func=SIGMOID)

        w_pairs = const.tile([P, V_PASSES, PACK, H], BF16, name="w_pairs")
        for g in range(V_PASSES):
            nc.sync.dma_start(
                out=w_pairs[:, g, :, :].rearrange("q (u e) c -> q u (e c)", e=2),
                in_=w[g * K_PASS : (g + 1) * K_PASS, :].rearrange("(u q e) c -> q u (e c)", u=2, e=2),
            )
        nc.sync.dma_start(out=hb_rows[0:2, :], in_=hb.rearrange("(u c) -> u c", u=2))
        nc.sync.dma_start(out=vb_rows[0:1, :], in_=vb.rearrange("(o c) -> o c", o=1))
        v_rows = []
        for c in range(CHUNKS):
            v_chunk = const.tile([P, CHUNK_TILES, V], BF16, name="v_rows%d" % c)
            size = CHUNK_TILES // 2 if c < 3 else CHUNK_TILES
            for j in range(0, CHUNK_TILES, size):
                first = c * CHUNK_TILES + j
                nc.sync.dma_start(out=v_chunk[:, j : j + size, :], in_=v_by_tile[:, first : first + size, :])
            v_rows.append(v_chunk)

        ident_f32 = const.tile([P, P], F32, name="ident_f32")
        make_identity(nc, ident_f32[:])

        w1_grouped = const.tile([P, V_PASSES, H * PACK], BF16, name="w1_grouped", align_bytes=64)
        w1_codes = const.tile([P, V_PASSES, H], U32, name="w1_codes", align_bytes=64)
        w1_scales = const.tile([P, V_PASSES, H], U8, name="w1_scales", align_bytes=64)
        for g in range(V_PASSES):
            for u in range(2):
                half = slice(u * 2 * P, (u + 1) * 2 * P)
                nc.vector.tensor_copy(
                    out=w1_grouped[:, g, u * 2 * P * PACK : (u + 1) * 2 * P * PACK].rearrange(
                        "p (e q t) -> p e q t", e=2, t=PACK
                    ),
                    in_=w_pairs[:, g, :, half].rearrange("p t (q e) -> p e q t", e=2),
                )
        for g in range(V_PASSES):
            nc.vector.quantize_mx(
                out=w1_codes[:, g, :].bitcast(FP8X4), scales=w1_scales[:, g, :], in_=w1_grouped[:, g, :]
            )

        w2_grouped = const.tile([P, V * PACK], BF16, name="w2_grouped", align_bytes=64)
        w2_codes = const.tile([P, V], U32, name="w2_codes", align_bytes=64)
        w2_scales = const.tile([P, V], U8, name="w2_scales", align_bytes=64)
        for x in range(2 * V_PASSES):
            g, r = divmod(x, 2)
            words = w_pairs[:, g, 2 * r : 2 * r + 2, :].bitcast(F32)
            w2_bank = psum.tile([P, 2, 2, P], F32, name="w2_bank", tag="bank")
            for e in range(2):
                for u in range(2):
                    nc.tensor.transpose(
                        out=w2_bank[:, e, u, :],
                        in_=words[:, e, u * P : (u + 1) * P],
                        identity=ident_f32[:],
                    )
            width = 2 * P * PACK
            nc.scalar.copy(
                out=w2_grouped[:, x * width : (x + 1) * width].bitcast(F32).rearrange("p (q e u) -> p q e u", e=2, u=2),
                in_=w2_bank[:].rearrange("p e u q -> p q e u"),
            )

        hb_bank = psum.tile([P, P], F32, name="hb_bank", tag="bank")
        nc.tensor.transpose(out=hb_bank[:], in_=hb_rows[:].bitcast(F32), identity=ident_f32[:])
        nc.scalar.copy(out=hb_col[:].bitcast(F32), in_=hb_bank[:, 0:2])

        def broadcast_vb():
            for n in range(V_HALVES):
                cols = slice(n * BANK, (n + 1) * BANK)
                vb_bank = psum.tile([P, BANK], F32, name="vb_bank", tag="bank")
                nc.tensor.matmul(out=vb_bank[:], lhsT=ones[:], rhs=vb_rows[:, cols], start=True, stop=True)
                nc.scalar.copy(out=vb_all[:, cols], in_=vb_bank[:])

        def quantise_w2(n):
            if not 0 <= n < V_HALVES:
                return
            nc.vector.quantize_mx(
                out=w2_codes[:, n * BANK : (n + 1) * BANK].bitcast(FP8X4),
                scales=w2_scales[:, n * BANK : (n + 1) * BANK],
                in_=w2_grouped[:, n * BANK * PACK : (n + 1) * BANK * PACK],
            )

        v_bank, v_grouped, v_codes, v_scales = {}, {}, {}, {}
        m1_bank, h_t, h_grouped, h_codes, h_scales = {}, {}, {}, {}, {}
        h_bank, h_out, m2_bank, r_out = {}, {}, {}, {}

        def transpose_v(x):
            if not 0 <= x < UNITS:
                return
            c, r = divmod(x, CHUNK_TILES)
            half, g = divmod(r, V_PASSES)
            words = v_rows[c][:].bitcast(F32)
            v_bank[x] = psum.tile([P, 2, 2 * P], F32, name="v_bank", tag="bank")
            for j in range(2):
                for u in range(2):
                    first = (2 * g + u) * P
                    nc.tensor.transpose(
                        out=v_bank[x][:, u, j * P : (j + 1) * P],
                        in_=words[:, 2 * half + j, first : first + P],
                        identity=ident_f32[:],
                    )

        def evacuate_v(x, engine_copy):
            if not 0 <= x < UNITS:
                return
            v_grouped[x] = ring.tile([P, 2 * P * PACK], BF16, name="v_grouped", tag="v_grouped", align_bytes=64)
            engine_copy(
                out=v_grouped[x][:].bitcast(F32).rearrange("p (n u) -> p n u", u=2),
                in_=v_bank[x][:].rearrange("p u n -> p n u"),
            )

        def quantise_v(x):
            if not 0 <= x < UNITS:
                return
            c, r = divmod(x, CHUNK_TILES)
            half, g = divmod(r, V_PASSES)
            if r == 0:
                v_codes[c] = ring.tile([P, V_PASSES, BANK], U32, name="v_codes", tag="v_codes", align_bytes=64)
                v_scales[c] = ring.tile([P, V_PASSES, BANK], U8, name="v_scales", tag="v_scales", align_bytes=64)
            cols = slice(half * 2 * P, (half + 1) * 2 * P)
            nc.vector.quantize_mx(
                out=v_codes[c][:, g, cols].bitcast(FP8X4), scales=v_scales[c][:, g, cols], in_=v_grouped[x][:]
            )

        def first_matmul(x):
            if not 0 <= x < UNITS:
                return
            c, t = divmod(x, H_BLOCKS)
            m1_bank[x] = psum.tile([P, BANK], F32, name="m1_bank", tag="bank")
            for g in range(V_PASSES):
                nc.tensor.matmul_mx(
                    out=m1_bank[x][:],
                    lhsT=w1_codes[:, g, t * P : (t + 1) * P].bitcast(FP8X4),
                    lhsT_scale=w1_scales[:, g, t * P : (t + 1) * P],
                    rhs=v_codes[c][:, g, :].bitcast(FP8X4),
                    rhs_scale=v_scales[c][:, g, :],
                    start=(g == 0),
                    stop=(g == V_PASSES - 1),
                )

        def hidden_sigmoid(x):
            if not 0 <= x < UNITS:
                return
            c, t = divmod(x, H_BLOCKS)
            if t == 0:
                h_t[c] = ring.tile([P, H_BLOCKS, BANK], F32, name="h_t", tag="h_t")
            nc.scalar.activation(out=h_t[c][:, t, :], in_=m1_bank[x][:], func=SIGMOID, bias=hb_col[:, t : t + 1])

        def regroup_h(x):
            if not 0 <= x < UNITS:
                return
            c, j = divmod(x, CHUNK_TILES)
            h_grouped[x] = ring.tile([P, P * PACK], BF16, name="h_grouped", tag="h_grouped", bufs=1, align_bytes=64)
            nc.gpsimd.tensor_scalar(
                out=h_grouped[x][:].rearrange("p (n t) -> p n t", t=PACK),
                in0=h_t[c][:, :, j * P : (j + 1) * P].rearrange("p t n -> p n t"),
                scalar1=1.0,
                scalar2=0.0,
                op0=MULT,
                op1=ADD,
            )

        def quantise_h(x):
            if not 0 <= x < UNITS:
                return
            h_codes[x] = ring.tile([P, P], U32, name="h_codes", tag="h_codes", align_bytes=64)
            h_scales[x] = ring.tile([P, P], U8, name="h_scales", tag="h_scales", align_bytes=64)
            nc.vector.quantize_mx(out=h_codes[x][:].bitcast(FP8X4), scales=h_scales[x][:], in_=h_grouped[x][:])

        def transpose_h(x):
            if not 0 <= x < UNITS:
                return
            c, j = divmod(x, CHUNK_TILES)
            h_bank[x] = psum.tile([P, H], F32, name="h_bank", tag="bank")
            for t in range(H_BLOCKS):
                nc.tensor.transpose(
                    out=h_bank[x][:, t * P : (t + 1) * P],
                    in_=h_t[c][:, t, j * P : (j + 1) * P],
                    identity=ident_f32[:],
                )

        def evacuate_h(x, engine_copy):
            if not 0 <= x < UNITS:
                return
            pair, j = divmod(x, 2)
            if j == 0:
                h_out[pair] = ring.tile([P, 2, H], F32, name="h_out", tag="h_out")
            engine_copy(
                out=h_out[pair][:, j, :].rearrange("p (u q e) -> p u q e", u=2, e=2),
                in_=h_bank[x][:].rearrange("p (u e q) -> p u q e", u=2, e=2),
            )
            if j == 1:
                nc.sync.dma_start(out=h_by_tile[:, 2 * pair : 2 * pair + 2, :], in_=h_out[pair][:])

        def second_matmul(x):
            if not 0 <= x < UNITS:
                return
            for n in range(V_HALVES):
                m2_bank[x, n] = psum.tile([P, BANK], F32, name="m2_bank", tag="bank")
                nc.tensor.matmul_mx(
                    out=m2_bank[x, n][:],
                    lhsT=h_codes[x][:].bitcast(FP8X4),
                    lhsT_scale=h_scales[x][:],
                    rhs=w2_codes[:, n * BANK : (n + 1) * BANK].bitcast(FP8X4),
                    rhs_scale=w2_scales[:, n * BANK : (n + 1) * BANK],
                    start=True,
                    stop=True,
                )

        def add_visible_bias(x):
            if not 0 <= x < UNITS:
                return
            r_out[x] = ring.tile([P, V], F32, name="r_out", tag="r_out", bufs=6)
            for n in range(V_HALVES):
                cols = slice(n * BANK, (n + 1) * BANK)
                nc.vector.tensor_tensor(out=r_out[x][:, cols], in0=m2_bank[x, n][:], in1=vb_all[:, cols], op=ADD)

        def visible_sigmoid(x):
            if not 0 <= x < UNITS:
                return
            nc.scalar.activation(out=r_out[x][:], in_=r_out[x][:], func=SIGMOID)
            nc.sync.dma_start(out=r_by_tile[:, x, :], in_=r_out[x][:])

        def vector_empties_v(x):
            return CHUNK_TILES <= x < FAST and x % 2 == 1

        for s in range(STEPS):
            scalar_has_time = s > step_of_m1(UNITS - 1)
            for x in units_at(step_of_v, s):
                transpose_v(x)
            for x in units_at(step_of_m2, s):
                transpose_h(x)
            for x in units_at(step_of_v, s):
                if not vector_empties_v(x):
                    evacuate_v(x, nc.scalar.copy)
            if not scalar_has_time:
                for x in units_at(step_of_m2, s):
                    evacuate_h(x, nc.vector.tensor_copy)
            if s == 1:
                broadcast_vb()
            for x in units_at(step_of_v, s - 1):
                quantise_v(x)
            quantise_w2(s - FIRST_W2_STEP)
            for x in units_at(step_of_m2, s + 1):
                quantise_h(x)
            for x in units_at(step_of_m1, s):
                first_matmul(x)
            for x in units_at(step_of_m2, s):
                second_matmul(x)
            for x in units_at(step_of_m1, s):
                hidden_sigmoid(x)
            if scalar_has_time:
                for x in units_at(step_of_m2, s):
                    evacuate_h(x, nc.scalar.copy)
            for x in units_at(step_of_m2, s - 1):
                visible_sigmoid(x)
            for x in units_at(step_of_v, s):
                if vector_empties_v(x):
                    evacuate_v(x, nc.vector.tensor_copy)
            for x in units_at(step_of_m2, s):
                add_visible_bias(x)
            for x in units_at(step_of_m2, s + 2):
                regroup_h(x)
